import numpy as np
import ml_dtypes


def mxq(x, axis, fmt="e4m3"):
    dtype, down = {"e4m3": (ml_dtypes.float8_e4m3fn, 7), "e5m2": (ml_dtypes.float8_e5m2, 14)}[fmt]
    v = np.moveaxis(np.asarray(x, np.float32).astype(ml_dtypes.bfloat16).astype(np.float64), axis, -1)
    blocks = v.reshape(v.shape[:-1] + (-1, 32))
    amax = np.abs(blocks).max(-1, keepdims=True)
    byte = np.maximum(np.where(amax > 0, np.frexp(amax)[1] - 1 + 127, 0) - down, 1)
    scale = np.exp2(byte - 127.0)
    codes = (blocks / scale).astype(np.float32).astype(dtype).astype(np.float64)
    return np.moveaxis((codes * scale).reshape(v.shape), -1, axis)


WIDE = False


def mx_kscale(k):
    if not WIDE:
        return np.ones(k)
    levels = np.array([10, -10, 5, -5, 0])
    a = np.random.permutation(np.resize(levels, k // 512 * 4)).reshape(k // 512, 4)
    idx = np.arange(k)
    return np.exp2(a[idx // 512, idx % 128 // 32])


BF16 = ml_dtypes.bfloat16


def bf(x):
    return np.asarray(x, np.float32).astype(BF16)


def f64(x):
    return np.asarray(x).astype(np.float64)


B, IN, NLVL, KLVL, C, CM, CO, OU, OV = 64, 256, 4, 1, 256, 1024, 256, 8, 8
NK = 2 ** KLVL
S = 2 ** (NLVL - KLVL)
KA, KB = 4 * C, 4 * CM


def patches(x):
    U, V, Bn, H, W, Cc = x.shape
    return x.reshape(U, V, Bn, H // 2, 2, W // 2, 2, Cc).swapaxes(4, 5).reshape(U, V, Bn * (H // 2) * (W // 2), 4 * Cc)


def node_conv(x, w, b):
    U, V, Bn, H, W, Cc = x.shape
    Co = w.shape[-1]
    y = (mxq(patches(x), 3, "e4m3") @ mxq(w.reshape(U, V, 4 * Cc, Co), 2, "e4m3")) + b[:, :, None, :]
    return np.maximum(y, 0.0).reshape(U, V, Bn, H // 2, W // 2, Co)


def setup_inputs():
    s = mx_kscale(KA).reshape(2, 2, C)
    t = mx_kscale(KB)[:CM]
    x = np.maximum(np.random.standard_normal((NK, NK, B, S, S, C)), 0.0) * np.tile(s, (S // 2, S // 2, 1))
    return {"x_leaf": bf(x),
            "f_first": bf(np.random.standard_normal((NK, NK, 2, 2, C, CM)) * np.sqrt(0.5 / C) / s[:, :, :, None] * t),
            "b_first": bf(np.random.standard_normal((NK, NK, CM)) * 0.2 * t),
            "f_second": bf(np.random.standard_normal((NK, NK, 2, 2, CM, CO)) * np.sqrt(0.5 / CM) / t[:, None]),
            "b_second": bf(np.random.standard_normal((NK, NK, CO)) * 0.2)}


def reference(x_leaf, f_first, b_first, f_second, b_second):
    h = node_conv(f64(x_leaf), f64(f_first), f64(b_first))
    return node_conv(h, f64(f_second), f64(b_second))

@@ -1,0 +1,261 @@
+from contextlib import ExitStack
+
+import concourse.mybir as mybir
+from concourse.masks import make_identity
+
+BF16 = mybir.dt.bfloat16
+F32 = mybir.dt.float32
+U32 = mybir.dt.uint32
+U8 = mybir.dt.uint8
+FP8X4 = mybir.dt.float8_e4m3fn_x4
+RELU = mybir.ActivationFunctionType.Relu
+ADD = mybir.AluOpType.add
+
+P = 128
+PACK = 4
+HALVES = 8
+HALF_SAMPLES = 32
+C_MID = 1024
+C_OUT = 256
+CHUNKS = C_MID // P
+COLS = 512
+RAW = 4096
+QUARTER = 512
+SET_WORDS = 4 * QUARTER
+LOADS_AHEAD = 3
+
+FLOPS = 2 * 4 * (1024 * 1024 * 1024 + 256 * 4096 * 256)
+
+
+def tile_butterflylayer2d_pb_t_kernel(tc, x_leaf, f_first, b_first, f_second, b_second, out):
+    nc = tc.nc
+    with ExitStack() as ctx:
+        ctx.enter_context(tc.manual_schedule())
+        consts = ctx.enter_context(tc.tile_pool(name="consts", bufs=1))
+        raw_pool = ctx.enter_context(tc.tile_pool(name="raw", bufs=3 * LOADS_AHEAD))
+        grouped_pool = ctx.enter_context(tc.tile_pool(name="grouped", bufs=4))
+        set_pool = ctx.enter_context(tc.tile_pool(name="sets", bufs=3))
+        code_pool = ctx.enter_context(tc.tile_pool(name="codes", bufs=2))
+        out_pool = ctx.enter_context(tc.tile_pool(name="outs", bufs=2))
+        psum_x = ctx.enter_context(tc.psum_pool(name="psum_x", bufs=4))
+        psum_h = ctx.enter_context(tc.psum_pool(name="psum_h", bufs=3))
+        psum_out = ctx.enter_context(tc.psum_pool(name="psum_out", bufs=1))
+
+        identity = consts.tile([P, P], F32)
+        make_identity(nc, identity[:])
+
+        bias_first = consts.tile([P, 4 * CHUNKS], BF16)
+        with nc.allow_non_contiguous_dma(reason="a 8 KiB bias in runs of 4 values"):
+            nc.scalar.dma_start(
+                out=bias_first[:].rearrange("w (n lo) -> w n lo", lo=4),
+                in_=b_first.rearrange("i j (hi w lo) -> w (i j hi) lo", hi=2, lo=4),
+            )
+        bias_second = consts.tile([P, 4 * C_OUT], BF16)
+
+        x_raw = {}
+        w_raw = {}
+        x_grouped = {}
+        w_grouped = {}
+        h_grouped = {}
+        x_mx = {}
+        w_mx = {}
+        h_mx = {}
+        acc_out = {}
+        summed = {}
+
+        def load(half):
+            i, j = divmod(half // 2, 2)
+            for piece in range(2):
+                rows = raw_pool.tile([P, RAW], BF16, tag="raw", name="w_rows")
+                if half % 2 == 0:
+                    nc.sync.dma_start(
+                        out=rows[:].rearrange("w (q r) -> w q r", q=2),
+                        in_=f_first[i, j, piece].rearrange("q (w e) o -> w q (e o)", e=2),
+                    )
+                else:
+                    nc.sync.dma_start(
+                        out=rows[:].rearrange("w (t r) -> w t r", t=PACK),
+                        in_=f_second[i, j].rearrange("p q (hi w lo) o -> hi w (p q) (lo o)", hi=2, lo=4)[piece],
+                    )
+                w_raw[(half, piece)] = rows
+                if piece == 0:
+                    first = (half % 2) * HALF_SAMPLES
+                    pixels = raw_pool.tile([P, RAW], BF16, tag="raw", name="pixels")
+                    nc.sync.dma_start(
+                        out=pixels[:],
+                        in_=x_leaf[i, j, first : first + HALF_SAMPLES].rearrange(
+                            "n (yh p) x c -> (n yh) (p x c)", p=2
+                        ),
+                    )
+                    x_raw[half] = pixels
+
+        def transpose_x(half):
+            words = x_raw[half][:].bitcast(F32)
+            for p in range(2):
+                grouped = grouped_pool.tile([P, PACK * COLS], BF16, tag="x_grouped", align_bytes=64)
+                x_grouped[(half, p)] = grouped
+                for x2 in range(2):
+                    bank = psum_x.tile([P, 4, P], F32, tag="x_bank")
+                    for a in range(4):
+                        pixel = 8 * p + 4 * x2 + a
+                        nc.tensor.transpose(bank[:, a, :], words[:, pixel * P : (pixel + 1) * P], identity[:])
+                    nc.scalar.copy(
+                        out=grouped[:]
+                        .bitcast(F32)
+                        .rearrange("w (s x2 p2 a) -> w x2 s p2 a", x2=2, p2=2, a=4)[:, x2],
+                        in_=bank[:].rearrange("w a (s p2) -> w s p2 a", p2=2),
+                    )
+
+        def quantise_x(half, p):
+            if p == 0:
+                codes = code_pool.tile([P, 2 * COLS], U32, tag="x_codes", align_bytes=64)
+                scales = code_pool.tile([P, 2 * COLS], U8, tag="x_scales", align_bytes=64)
+                x_mx[half] = (codes, scales)
+            codes, scales = x_mx[half]
+            cols = slice(p * COLS, (p + 1) * COLS)
+            nc.vector.quantize_mx(
+                out=codes[:, cols].bitcast(FP8X4), scales=scales[:, cols], in_=x_grouped[(half, p)][:]
+            )
+
+        def regroup_w(w_set, quarter):
+            grouped = grouped_pool.tile([P, PACK * QUARTER], BF16, tag="w_grouped", align_bytes=64)
+            w_grouped[quarter] = grouped
+            rows = w_raw[(w_set, quarter // 2)][:].rearrange("w (t h c i) -> w h c t i", t=PACK, h=2, i=4)
+            if w_set % 2 == 0:
+                columns = grouped[:].rearrange("w (i c t) -> w c t i", i=4, t=PACK)
+            else:
+                columns = grouped[:].rearrange("w (c i t) -> w c t i", i=4, t=PACK)
+            nc.vector.tensor_copy(out=columns, in_=rows[:, quarter % 2])
+
+        def quantise_w(w_set, quarter):
+            if quarter == 0:
+                codes = set_pool.tile([P, SET_WORDS], U32, tag="w_codes", align_bytes=64)
+                scales = set_pool.tile([P, SET_WORDS], U8, tag="w_scales", align_bytes=64)
+                w_mx[w_set] = (codes, scales)
+            codes, scales = w_mx[w_set]
+            cols = slice(quarter * QUARTER, (quarter + 1) * QUARTER)
+            nc.vector.quantize_mx(
+                out=codes[:, cols].bitcast(FP8X4), scales=scales[:, cols], in_=w_grouped[quarter][:]
+            )
+
+        def first_conv(half, chunk):
+            node = half // 2
+            w_codes, w_scales = w_mx[2 * node]
+            x_codes, x_scales = x_mx[half]
+            acc = psum_h.tile([P, COLS], F32, tag="acc_h")
+            for p in range(2):
+                w_cols = slice(p * C_MID + chunk * P, p * C_MID + (chunk + 1) * P)
+                x_cols = slice(p * COLS, (p + 1) * COLS)
+                nc.tensor.matmul_mx(
+                    out=acc[:],
+                    lhsT=w_codes[:, w_cols].bitcast(FP8X4),
+                    lhsT_scale=w_scales[:, w_cols],
+                    rhs=x_codes[:, x_cols].bitcast(FP8X4),
+                    rhs_scale=x_scales[:, x_cols],
+                    start=(p == 0),
+                    stop=(p == 1),
+                )
+            if chunk % 4 == 0:
+                h_grouped[(half, chunk // 4)] = grouped_pool.tile(
+                    [P, 4, COLS], BF16, tag="h_grouped", name="h_grouped", align_bytes=64
+                )
+            nc.scalar.activation(
+                out=h_grouped[(half, chunk // 4)][:, chunk % 4, :],
+                in_=acc[:],
+                func=RELU,
+                bias=bias_first[:, node * CHUNKS + chunk : node * CHUNKS + chunk + 1],
+                scale=1.0,
+            )
+
+        def quantise_h(half, group):
+            if group == 0:
+                codes = code_pool.tile([P, CHUNKS * P], U32, tag="h_codes", align_bytes=64)
+                scales = code_pool.tile([P, CHUNKS * P], U8, tag="h_scales", align_bytes=64)
+                h_mx[half] = (codes, scales)
+            codes, scales = h_mx[half]
+            cols = slice(group * 4 * P, (group + 1) * 4 * P)
+            nc.vector.quantize_mx(
+                out=codes[:, cols].bitcast(FP8X4),
+                scales=scales[:, cols],
+                in_=h_grouped[(half, group)][:].rearrange("w m c -> w (m c)"),
+            )
+
+        def second_conv(half):
+            h_codes, h_scales = h_mx[half]
+            w_codes, w_scales = w_mx[2 * (half // 2) + 1]
+            acc = psum_out.tile([P, C_OUT], F32, tag="acc_out")
+            acc_out[half] = acc
+            for chunk in range(CHUNKS):
+                h_cols = slice(chunk * P, (chunk + 1) * P)
+                w_cols = slice(chunk * C_OUT, (chunk + 1) * C_OUT)
+                nc.tensor.matmul_mx(
+                    out=acc[:],
+                    lhsT=h_codes[:, h_cols].bitcast(FP8X4),
+                    lhsT_scale=h_scales[:, h_cols],
+                    rhs=w_codes[:, w_cols].bitcast(FP8X4),
+                    rhs_scale=w_scales[:, w_cols],
+                    start=(chunk == 0),
+                    stop=(chunk == CHUNKS - 1),
+                )
+
+        def add_bias(half):
+            node = half // 2
+            summed[half] = out_pool.tile([P, C_OUT], F32, tag="summed", name="summed")
+            nc.vector.tensor_tensor(
+                out=summed[half][:],
+                in0=acc_out[half][:],
+                in1=bias_second[:, node * C_OUT : (node + 1) * C_OUT],
+                op=ADD,
+            )
+
+        def relu_and_store(half):
+            i, j = divmod(half // 2, 2)
+            first = (half % 2) * HALF_SAMPLES
+            result = out_pool.tile([P, C_OUT], F32, tag="result")
+            nc.scalar.activation(out=result[:], in_=summed[half][:], func=RELU)
+            nc.scalar.dma_start(
+                out=out[i, j, first : first + HALF_SAMPLES].rearrange("n y x c -> (n y x) c"), in_=result[:]
+            )
+
+        load(0)
+        nc.sync.dma_start(out=bias_second[:], in_=b_second.rearrange("i j c -> (i j c)").partition_broadcast(P))
+        for half in range(1, LOADS_AHEAD):
+            load(half)
+        for step in range(HALVES + 2):
+            preparing = step < HALVES
+            convolving = 1 <= step <= HALVES
+            finishing = step >= 2
+            if finishing:
+                quantise_h(step - 2, 1)
+            if preparing:
+                transpose_x(step)
+            if finishing:
+                second_conv(step - 2)
+            if preparing:
+                regroup_w(step, 0)
+                regroup_w(step, 1)
+            if finishing:
+                add_bias(step - 2)
+            if preparing:
+                quantise_w(step, 0)
+                quantise_x(step, 0)
+                quantise_w(step, 1)
+                quantise_x(step, 1)
+            if convolving:
+                for chunk in range(4):
+                    first_conv(step - 1, chunk)
+            if finishing:
+                relu_and_store(step - 2)
+            if preparing:
+                regroup_w(step, 2)
+                regroup_w(step, 3)
+                if step + LOADS_AHEAD < HALVES:
+                    load(step + LOADS_AHEAD)
+                quantise_w(step, 2)
+            if convolving:
+                quantise_h(step - 1, 0)
+            if preparing:
+                quantise_w(step, 3)
+            if convolving:
+                for chunk in range(4, CHUNKS):
+                    first_conv(step - 1, chunk)

@@ -23,6 +23,7 @@ RAW = 4096
 QUARTER = 512
 SET_WORDS = 4 * QUARTER
 LOADS_AHEAD = 3
+SCALAR_QUARTER = 1
 
 FLOPS = 2 * 4 * (1024 * 1024 * 1024 + 256 * 4096 * 256)
 
@@ -50,7 +51,16 @@ def tile_butterflylayer2d_pb_t_kernel(tc, x_leaf, f_first, b_first, f_second, b_
                 out=bias_first[:].rearrange("w (n lo) -> w n lo", lo=4),
                 in_=b_first.rearrange("i j (hi w lo) -> w (i j hi) lo", hi=2, lo=4),
             )
-        bias_second = consts.tile([P, 4 * C_OUT], BF16)
+        ones = consts.tile([P, P], BF16)
+        nc.vector.memset(ones[:], 1.0)
+        bias_row = consts.tile([P, 4 * C_OUT], BF16)
+        nc.vector.memset(bias_row[:], 0.0)
+        nc.scalar.dma_start(out=bias_row[0:1, :], in_=b_second.rearrange("(one i) j c -> one (i j c)", one=1))
+        bias_second = consts.tile([P, 4 * C_OUT], F32)
+        for cols in (slice(0, COLS), slice(COLS, 2 * COLS)):
+            spread = psum_h.tile([P, COLS], F32, tag="acc_h")
+            nc.tensor.matmul(out=spread[:], lhsT=ones[:], rhs=bias_row[:, cols], start=True, stop=True)
+            nc.scalar.copy(out=bias_second[:, cols], in_=spread[:])
 
         x_raw = {}
         w_raw = {}
@@ -65,8 +75,15 @@ def tile_butterflylayer2d_pb_t_kernel(tc, x_leaf, f_first, b_first, f_second, b_
 
         def load(half):
             i, j = divmod(half // 2, 2)
+            first = (half % 2) * HALF_SAMPLES
+            pixels = raw_pool.tile([P, RAW], BF16, tag="raw")
+            nc.sync.dma_start(
+                out=pixels[:],
+                in_=x_leaf[i, j, first : first + HALF_SAMPLES].rearrange("n (yh p) x c -> (n yh) (p x c)", p=2),
+            )
+            x_raw[half] = pixels
             for piece in range(2):
-                rows = raw_pool.tile([P, RAW], BF16, tag="raw", name="w_rows")
+                rows = raw_pool.tile([P, RAW], BF16, tag="raw")
                 if half % 2 == 0:
                     nc.sync.dma_start(
                         out=rows[:].rearrange("w (q r) -> w q r", q=2),
@@ -78,16 +95,6 @@ def tile_butterflylayer2d_pb_t_kernel(tc, x_leaf, f_first, b_first, f_second, b_
                         in_=f_second[i, j].rearrange("p q (hi w lo) o -> hi w (p q) (lo o)", hi=2, lo=4)[piece],
                     )
                 w_raw[(half, piece)] = rows
-                if piece == 0:
-                    first = (half % 2) * HALF_SAMPLES
-                    pixels = raw_pool.tile([P, RAW], BF16, tag="raw", name="pixels")
-                    nc.sync.dma_start(
-                        out=pixels[:],
-                        in_=x_leaf[i, j, first : first + HALF_SAMPLES].rearrange(
-                            "n (yh p) x c -> (n yh) (p x c)", p=2
-                        ),
-                    )
-                    x_raw[half] = pixels
 
         def transpose_x(half):
             words = x_raw[half][:].bitcast(F32)
@@ -125,7 +132,10 @@ def tile_butterflylayer2d_pb_t_kernel(tc, x_leaf, f_first, b_first, f_second, b_
                 columns = grouped[:].rearrange("w (i c t) -> w c t i", i=4, t=PACK)
             else:
                 columns = grouped[:].rearrange("w (c i t) -> w c t i", i=4, t=PACK)
-            nc.vector.tensor_copy(out=columns, in_=rows[:, quarter % 2])
+            if quarter == SCALAR_QUARTER:
+                nc.scalar.copy(out=columns, in_=rows[:, quarter % 2])
+            else:
+                nc.vector.tensor_copy(out=columns, in_=rows[:, quarter % 2])
 
         def quantise_w(w_set, quarter):
             if quarter == 0:
@@ -217,9 +227,7 @@ def tile_butterflylayer2d_pb_t_kernel(tc, x_leaf, f_first, b_first, f_second, b_
                 out=out[i, j, first : first + HALF_SAMPLES].rearrange("n y x c -> (n y x) c"), in_=result[:]
             )
 
-        load(0)
-        nc.sync.dma_start(out=bias_second[:], in_=b_second.rearrange("i j c -> (i j c)").partition_broadcast(P))
-        for half in range(1, LOADS_AHEAD):
+        for half in range(LOADS_AHEAD):
             load(half)
         for step in range(HALVES + 2):
             preparing = step < HALVES
@@ -228,30 +236,30 @@ def tile_butterflylayer2d_pb_t_kernel(tc, x_leaf, f_first, b_first, f_second, b_
             if finishing:
                 quantise_h(step - 2, 1)
             if preparing:
+                regroup_w(step, 1)
                 transpose_x(step)
             if finishing:
                 second_conv(step - 2)
             if preparing:
                 regroup_w(step, 0)
-                regroup_w(step, 1)
+                regroup_w(step, 2)
             if finishing:
                 add_bias(step - 2)
             if preparing:
                 quantise_w(step, 0)
                 quantise_x(step, 0)
-                quantise_w(step, 1)
+                quantise_w(step, 2)
                 quantise_x(step, 1)
+                quantise_w(step, 1)
             if convolving:
                 for chunk in range(4):
                     first_conv(step - 1, chunk)
             if finishing:
                 relu_and_store(step - 2)
             if preparing:
-                regroup_w(step, 2)
                 regroup_w(step, 3)
                 if step + LOADS_AHEAD < HALVES:
                     load(step + LOADS_AHEAD)
-                quantise_w(step, 2)
             if convolving:
                 quantise_h(step - 1, 0)
             if preparing:

@@ -31,7 +31,6 @@ FLOPS = 2 * 4 * (1024 * 1024 * 1024 + 256 * 4096 * 256)
 def tile_butterflylayer2d_pb_t_kernel(tc, x_leaf, f_first, b_first, f_second, b_second, out):
     nc = tc.nc
     with ExitStack() as ctx:
-        ctx.enter_context(tc.manual_schedule())
         consts = ctx.enter_context(tc.tile_pool(name="consts", bufs=1))
         raw_pool = ctx.enter_context(tc.tile_pool(name="raw", bufs=3 * LOADS_AHEAD))
         grouped_pool = ctx.enter_context(tc.tile_pool(name="grouped", bufs=4))
@@ -56,11 +55,6 @@ def tile_butterflylayer2d_pb_t_kernel(tc, x_leaf, f_first, b_first, f_second, b_
         bias_row = consts.tile([P, 4 * C_OUT], BF16)
         nc.vector.memset(bias_row[:], 0.0)
         nc.scalar.dma_start(out=bias_row[0:1, :], in_=b_second.rearrange("(one i) j c -> one (i j c)", one=1))
-        bias_second = consts.tile([P, 4 * C_OUT], F32)
-        for cols in (slice(0, COLS), slice(COLS, 2 * COLS)):
-            spread = psum_h.tile([P, COLS], F32, tag="acc_h")
-            nc.tensor.matmul(out=spread[:], lhsT=ones[:], rhs=bias_row[:, cols], start=True, stop=True)
-            nc.scalar.copy(out=bias_second[:, cols], in_=spread[:])
 
         x_raw = {}
         w_raw = {}
@@ -70,6 +64,7 @@ def tile_butterflylayer2d_pb_t_kernel(tc, x_leaf, f_first, b_first, f_second, b_
         x_mx = {}
         w_mx = {}
         h_mx = {}
+        bias_second = {}
         acc_out = {}
         summed = {}
 
@@ -190,6 +185,18 @@ def tile_butterflylayer2d_pb_t_kernel(tc, x_leaf, f_first, b_first, f_second, b_
                 in_=h_grouped[(half, group)][:].rearrange("w m c -> w (m c)"),
             )
 
+        def spread_bias(node):
+            spread = psum_h.tile([P, COLS], F32, tag="acc_h")
+            nc.tensor.matmul(
+                out=spread[:, :C_OUT],
+                lhsT=ones[:],
+                rhs=bias_row[:, node * C_OUT : (node + 1) * C_OUT],
+                start=True,
+                stop=True,
+            )
+            bias_second[node] = out_pool.tile([P, C_OUT], F32, tag="bias_second", name="bias_second")
+            nc.scalar.copy(out=bias_second[node][:], in_=spread[:, :C_OUT])
+
         def second_conv(half):
             h_codes, h_scales = h_mx[half]
             w_codes, w_scales = w_mx[2 * (half // 2) + 1]
@@ -214,7 +221,7 @@ def tile_butterflylayer2d_pb_t_kernel(tc, x_leaf, f_first, b_first, f_second, b_
             nc.vector.tensor_tensor(
                 out=summed[half][:],
                 in0=acc_out[half][:],
-                in1=bias_second[:, node * C_OUT : (node + 1) * C_OUT],
+                in1=bias_second[node][:],
                 op=ADD,
             )
 
@@ -239,18 +246,19 @@ def tile_butterflylayer2d_pb_t_kernel(tc, x_leaf, f_first, b_first, f_second, b_
                 regroup_w(step, 1)
                 transpose_x(step)
             if finishing:
+                if step % 2 == 0:
+                    spread_bias((step - 2) // 2)
                 second_conv(step - 2)
             if preparing:
                 regroup_w(step, 0)
                 regroup_w(step, 2)
-            if finishing:
-                add_bias(step - 2)
-            if preparing:
                 quantise_w(step, 0)
                 quantise_x(step, 0)
                 quantise_w(step, 2)
                 quantise_x(step, 1)
                 quantise_w(step, 1)
+            if finishing:
+                add_bias(step - 2)
             if convolving:
                 for chunk in range(4):
                     first_conv(step - 1, chunk)

@@ -23,7 +23,8 @@ RAW = 4096
 QUARTER = 512
 SET_WORDS = 4 * QUARTER
 LOADS_AHEAD = 3
-SCALAR_QUARTER = 1
+SHARED_QUARTER = 1
+SCALAR_GROUPS = 96
 
 FLOPS = 2 * 4 * (1024 * 1024 * 1024 + 256 * 4096 * 256)
 
@@ -37,8 +38,8 @@ def tile_butterflylayer2d_pb_t_kernel(tc, x_leaf, f_first, b_first, f_second, b_
         set_pool = ctx.enter_context(tc.tile_pool(name="sets", bufs=3))
         code_pool = ctx.enter_context(tc.tile_pool(name="codes", bufs=2))
         out_pool = ctx.enter_context(tc.tile_pool(name="outs", bufs=2))
-        psum_x = ctx.enter_context(tc.psum_pool(name="psum_x", bufs=4))
-        psum_h = ctx.enter_context(tc.psum_pool(name="psum_h", bufs=3))
+        psum_x = ctx.enter_context(tc.psum_pool(name="psum_x", bufs=2))
+        psum_h = ctx.enter_context(tc.psum_pool(name="psum_h", bufs=5))
         psum_out = ctx.enter_context(tc.psum_pool(name="psum_out", bufs=1))
 
         identity = consts.tile([P, P], F32)
@@ -127,10 +128,12 @@ def tile_butterflylayer2d_pb_t_kernel(tc, x_leaf, f_first, b_first, f_second, b_
                 columns = grouped[:].rearrange("w (i c t) -> w c t i", i=4, t=PACK)
             else:
                 columns = grouped[:].rearrange("w (c i t) -> w c t i", i=4, t=PACK)
-            if quarter == SCALAR_QUARTER:
-                nc.scalar.copy(out=columns, in_=rows[:, quarter % 2])
+            source = rows[:, quarter % 2]
+            if quarter == SHARED_QUARTER:
+                nc.scalar.copy(out=columns[:, :SCALAR_GROUPS], in_=source[:, :SCALAR_GROUPS])
+                nc.vector.tensor_copy(out=columns[:, SCALAR_GROUPS:], in_=source[:, SCALAR_GROUPS:])
             else:
-                nc.vector.tensor_copy(out=columns, in_=rows[:, quarter % 2])
+                nc.vector.tensor_copy(out=columns, in_=source)
 
         def quantise_w(w_set, quarter):
             if quarter == 0:

@@ -71,13 +71,6 @@ def tile_butterflylayer2d_pb_t_kernel(tc, x_leaf, f_first, b_first, f_second, b_
 
         def load(half):
             i, j = divmod(half // 2, 2)
-            first = (half % 2) * HALF_SAMPLES
-            pixels = raw_pool.tile([P, RAW], BF16, tag="raw")
-            nc.sync.dma_start(
-                out=pixels[:],
-                in_=x_leaf[i, j, first : first + HALF_SAMPLES].rearrange("n (yh p) x c -> (n yh) (p x c)", p=2),
-            )
-            x_raw[half] = pixels
             for piece in range(2):
                 rows = raw_pool.tile([P, RAW], BF16, tag="raw")
                 if half % 2 == 0:
@@ -91,6 +84,14 @@ def tile_butterflylayer2d_pb_t_kernel(tc, x_leaf, f_first, b_first, f_second, b_
                         in_=f_second[i, j].rearrange("p q (hi w lo) o -> hi w (p q) (lo o)", hi=2, lo=4)[piece],
                     )
                 w_raw[(half, piece)] = rows
+                if piece == 0:
+                    first = (half % 2) * HALF_SAMPLES
+                    pixels = raw_pool.tile([P, RAW], BF16, tag="raw")
+                    nc.sync.dma_start(
+                        out=pixels[:],
+                        in_=x_leaf[i, j, first : first + HALF_SAMPLES].rearrange("n (yh p) x c -> (n yh) (p x c)", p=2),
+                    )
+                    x_raw[half] = pixels
 
         def transpose_x(half):
             words = x_raw[half][:].bitcast(F32)
@@ -240,41 +241,27 @@ def tile_butterflylayer2d_pb_t_kernel(tc, x_leaf, f_first, b_first, f_second, b_
         for half in range(LOADS_AHEAD):
             load(half)
         for step in range(HALVES + 2):
-            preparing = step < HALVES
-            convolving = 1 <= step <= HALVES
-            finishing = step >= 2
-            if finishing:
-                quantise_h(step - 2, 1)
-            if preparing:
-                regroup_w(step, 1)
+            if step >= 2:
+                half = step - 2
+                quantise_h(half, 1)
+                if half % 2 == 0:
+                    spread_bias(half // 2)
+                second_conv(half)
+                add_bias(half)
+                relu_and_store(half)
+            if step < HALVES:
                 transpose_x(step)
-            if finishing:
-                if step % 2 == 0:
-                    spread_bias((step - 2) // 2)
-                second_conv(step - 2)
-            if preparing:
-                regroup_w(step, 0)
-                regroup_w(step, 2)
-                quantise_w(step, 0)
-                quantise_x(step, 0)
-                quantise_w(step, 2)
-                quantise_x(step, 1)
-                quantise_w(step, 1)
-            if finishing:
-                add_bias(step - 2)
-            if convolving:
-                for chunk in range(4):
-                    first_conv(step - 1, chunk)
-            if finishing:
-                relu_and_store(step - 2)
-            if preparing:
-                regroup_w(step, 3)
+                for quarter in range(4):
+                    regroup_w(step, quarter)
+                for p in range(2):
+                    quantise_x(step, p)
+                for quarter in range(4):
+                    quantise_w(step, quarter)
                 if step + LOADS_AHEAD < HALVES:
                     load(step + LOADS_AHEAD)
-            if convolving:
-                quantise_h(step - 1, 0)
-            if preparing:
-                quantise_w(step, 3)
-            if convolving:
-                for chunk in range(4, CHUNKS):
-                    first_conv(step - 1, chunk)
+            if 1 <= step <= HALVES:
+                half = step - 1
+                for chunk in range(CHUNKS):
+                    first_conv(half, chunk)
+                    if chunk == 3:
+                        quantise_h(half, 0)

@@ -13,20 +13,23 @@ ADD = mybir.AluOpType.add
 
 P = 128
 PACK = 4
-HALVES = 8
+NODES = 4
+HALVES = 2 * NODES
 HALF_SAMPLES = 32
 C_MID = 1024
 C_OUT = 256
 CHUNKS = C_MID // P
+GROUP = 4
 COLS = 512
 RAW = 4096
+QUARTERS = 4
 QUARTER = 512
-SET_WORDS = 4 * QUARTER
+RUN = 4
 LOADS_AHEAD = 3
 SHARED_QUARTER = 1
 SCALAR_GROUPS = 96
 
-FLOPS = 2 * 4 * (1024 * 1024 * 1024 + 256 * 4096 * 256)
+FLOPS = 2 * NODES * (1024 * 1024 * 1024 + 256 * 4096 * 256)
 
 
 def tile_butterflylayer2d_pb_t_kernel(tc, x_leaf, f_first, b_first, f_second, b_second, out):
@@ -34,7 +37,7 @@ def tile_butterflylayer2d_pb_t_kernel(tc, x_leaf, f_first, b_first, f_second, b_
     with ExitStack() as ctx:
         consts = ctx.enter_context(tc.tile_pool(name="consts", bufs=1))
         raw_pool = ctx.enter_context(tc.tile_pool(name="raw", bufs=3 * LOADS_AHEAD))
-        grouped_pool = ctx.enter_context(tc.tile_pool(name="grouped", bufs=4))
+        grouped_pool = ctx.enter_context(tc.tile_pool(name="grouped", bufs=QUARTERS))
         set_pool = ctx.enter_context(tc.tile_pool(name="sets", bufs=3))
         code_pool = ctx.enter_context(tc.tile_pool(name="codes", bufs=2))
         out_pool = ctx.enter_context(tc.tile_pool(name="outs", bufs=2))
@@ -45,17 +48,17 @@ def tile_butterflylayer2d_pb_t_kernel(tc, x_leaf, f_first, b_first, f_second, b_
         identity = consts.tile([P, P], F32)
         make_identity(nc, identity[:])
 
-        bias_first = consts.tile([P, 4 * CHUNKS], BF16)
+        bias_first = consts.tile([P, NODES * CHUNKS], BF16)
         with nc.allow_non_contiguous_dma(reason="a 8 KiB bias in runs of 4 values"):
             nc.scalar.dma_start(
-                out=bias_first[:].rearrange("w (n lo) -> w n lo", lo=4),
-                in_=b_first.rearrange("i j (hi w lo) -> w (i j hi) lo", hi=2, lo=4),
+                out=bias_first[:].rearrange("k (g lo) -> k g lo", lo=4),
+                in_=b_first.rearrange("r s (hi k lo) -> k (r s hi) lo", hi=2, lo=4),
             )
         ones = consts.tile([P, P], BF16)
         nc.vector.memset(ones[:], 1.0)
-        bias_row = consts.tile([P, 4 * C_OUT], BF16)
+        bias_row = consts.tile([P, NODES * C_OUT], BF16)
         nc.vector.memset(bias_row[:], 0.0)
-        nc.scalar.dma_start(out=bias_row[0:1, :], in_=b_second.rearrange("(one i) j c -> one (i j c)", one=1))
+        nc.scalar.dma_start(out=bias_row[0:1, :], in_=b_second.rearrange("(one r) s o -> one (r s o)", one=1))
 
         x_raw = {}
         w_raw = {}
@@ -69,45 +72,55 @@ def tile_butterflylayer2d_pb_t_kernel(tc, x_leaf, f_first, b_first, f_second, b_
         acc_out = {}
         summed = {}
 
+        def load_weights(w_set, piece):
+            node_row, node_col = divmod(w_set // 2, 2)
+            rows = raw_pool.tile([P, RAW], BF16, tag="raw")
+            if w_set % 2 == 0:
+                nc.sync.dma_start(
+                    out=rows[:].rearrange("k (q r) -> k q r", q=2),
+                    in_=f_first[node_row, node_col, piece].rearrange("q (k e) m -> k q (e m)", e=2),
+                )
+            else:
+                nc.sync.dma_start(
+                    out=rows[:].rearrange("k (t r) -> k t r", t=PACK),
+                    in_=f_second[node_row, node_col].rearrange(
+                        "u v (hi k lo) o -> hi k (u v) (lo o)", hi=2, lo=4
+                    )[piece],
+                )
+            w_raw[(w_set, piece)] = rows
+
+        def load_x(half):
+            node_row, node_col = divmod(half // 2, 2)
+            first = (half % 2) * HALF_SAMPLES
+            pixels = raw_pool.tile([P, RAW], BF16, tag="raw")
+            nc.sync.dma_start(
+                out=pixels[:],
+                in_=x_leaf[node_row, node_col, first : first + HALF_SAMPLES].rearrange(
+                    "n (Y p) X c -> (n Y) (p X c)", p=2
+                ),
+            )
+            x_raw[half] = pixels
+
         def load(half):
-            i, j = divmod(half // 2, 2)
-            for piece in range(2):
-                rows = raw_pool.tile([P, RAW], BF16, tag="raw")
-                if half % 2 == 0:
-                    nc.sync.dma_start(
-                        out=rows[:].rearrange("w (q r) -> w q r", q=2),
-                        in_=f_first[i, j, piece].rearrange("q (w e) o -> w q (e o)", e=2),
-                    )
-                else:
-                    nc.sync.dma_start(
-                        out=rows[:].rearrange("w (t r) -> w t r", t=PACK),
-                        in_=f_second[i, j].rearrange("p q (hi w lo) o -> hi w (p q) (lo o)", hi=2, lo=4)[piece],
-                    )
-                w_raw[(half, piece)] = rows
-                if piece == 0:
-                    first = (half % 2) * HALF_SAMPLES
-                    pixels = raw_pool.tile([P, RAW], BF16, tag="raw")
-                    nc.sync.dma_start(
-                        out=pixels[:],
-                        in_=x_leaf[i, j, first : first + HALF_SAMPLES].rearrange("n (yh p) x c -> (n yh) (p x c)", p=2),
-                    )
-                    x_raw[half] = pixels
+            load_weights(half, 0)
+            load_x(half)
+            load_weights(half, 1)
 
         def transpose_x(half):
             words = x_raw[half][:].bitcast(F32)
             for p in range(2):
                 grouped = grouped_pool.tile([P, PACK * COLS], BF16, tag="x_grouped", align_bytes=64)
                 x_grouped[(half, p)] = grouped
-                for x2 in range(2):
+                for x in range(2):
                     bank = psum_x.tile([P, 4, P], F32, tag="x_bank")
                     for a in range(4):
-                        pixel = 8 * p + 4 * x2 + a
+                        pixel = 8 * p + 4 * x + a
                         nc.tensor.transpose(bank[:, a, :], words[:, pixel * P : (pixel + 1) * P], identity[:])
                     nc.scalar.copy(
                         out=grouped[:]
                         .bitcast(F32)
-                        .rearrange("w (s x2 p2 a) -> w x2 s p2 a", x2=2, p2=2, a=4)[:, x2],
-                        in_=bank[:].rearrange("w a (s p2) -> w s p2 a", p2=2),
+                        .rearrange("k (ny x u a) -> k x ny u a", x=2, u=2, a=4)[:, x],
+                        in_=bank[:].rearrange("k a (ny u) -> k ny u a", u=2),
                     )
 
         def quantise_x(half, p):
@@ -124,11 +137,11 @@ def tile_butterflylayer2d_pb_t_kernel(tc, x_leaf, f_first, b_first, f_second, b_
         def regroup_w(w_set, quarter):
             grouped = grouped_pool.tile([P, PACK * QUARTER], BF16, tag="w_grouped", align_bytes=64)
             w_grouped[quarter] = grouped
-            rows = w_raw[(w_set, quarter // 2)][:].rearrange("w (t h c i) -> w h c t i", t=PACK, h=2, i=4)
+            rows = w_raw[(w_set, quarter // 2)][:].rearrange("k (t h g i) -> k h g t i", t=PACK, h=2, i=RUN)
             if w_set % 2 == 0:
-                columns = grouped[:].rearrange("w (i c t) -> w c t i", i=4, t=PACK)
+                columns = grouped[:].rearrange("k (i g t) -> k g t i", i=RUN, t=PACK)
             else:
-                columns = grouped[:].rearrange("w (c i t) -> w c t i", i=4, t=PACK)
+                columns = grouped[:].rearrange("k (g i t) -> k g t i", i=RUN, t=PACK)
             source = rows[:, quarter % 2]
             if quarter == SHARED_QUARTER:
                 nc.scalar.copy(out=columns[:, :SCALAR_GROUPS], in_=source[:, :SCALAR_GROUPS])
@@ -138,8 +151,8 @@ def tile_butterflylayer2d_pb_t_kernel(tc, x_leaf, f_first, b_first, f_second, b_
 
         def quantise_w(w_set, quarter):
             if quarter == 0:
-                codes = set_pool.tile([P, SET_WORDS], U32, tag="w_codes", align_bytes=64)
-                scales = set_pool.tile([P, SET_WORDS], U8, tag="w_scales", align_bytes=64)
+                codes = set_pool.tile([P, QUARTERS * QUARTER], U32, tag="w_codes", align_bytes=64)
+                scales = set_pool.tile([P, QUARTERS * QUARTER], U8, tag="w_scales", align_bytes=64)
                 w_mx[w_set] = (codes, scales)
             codes, scales = w_mx[w_set]
             cols = slice(quarter * QUARTER, (quarter + 1) * QUARTER)
@@ -164,12 +177,12 @@ def tile_butterflylayer2d_pb_t_kernel(tc, x_leaf, f_first, b_first, f_second, b_
                     start=(p == 0),
                     stop=(p == 1),
                 )
-            if chunk % 4 == 0:
-                h_grouped[(half, chunk // 4)] = grouped_pool.tile(
-                    [P, 4, COLS], BF16, tag="h_grouped", name="h_grouped", align_bytes=64
+            if chunk % GROUP == 0:
+                h_grouped[(half, chunk // GROUP)] = grouped_pool.tile(
+                    [P, GROUP, COLS], BF16, tag="h_grouped", name="h_grouped", align_bytes=64
                 )
             nc.scalar.activation(
-                out=h_grouped[(half, chunk // 4)][:, chunk % 4, :],
+                out=h_grouped[(half, chunk // GROUP)][:, chunk % GROUP, :],
                 in_=acc[:],
                 func=RELU,
                 bias=bias_first[:, node * CHUNKS + chunk : node * CHUNKS + chunk + 1],
@@ -182,11 +195,11 @@ def tile_butterflylayer2d_pb_t_kernel(tc, x_leaf, f_first, b_first, f_second, b_
                 scales = code_pool.tile([P, CHUNKS * P], U8, tag="h_scales", align_bytes=64)
                 h_mx[half] = (codes, scales)
             codes, scales = h_mx[half]
-            cols = slice(group * 4 * P, (group + 1) * 4 * P)
+            cols = slice(group * GROUP * P, (group + 1) * GROUP * P)
             nc.vector.quantize_mx(
                 out=codes[:, cols].bitcast(FP8X4),
                 scales=scales[:, cols],
-                in_=h_grouped[(half, group)][:].rearrange("w m c -> w (m c)"),
+                in_=h_grouped[(half, group)][:].rearrange("k chunk col -> k (chunk col)"),
             )
 
         def spread_bias(node):
@@ -230,38 +243,53 @@ def tile_butterflylayer2d_pb_t_kernel(tc, x_leaf, f_first, b_first, f_second, b_
             )
 
         def relu_and_store(half):
-            i, j = divmod(half // 2, 2)
+            node_row, node_col = divmod(half // 2, 2)
             first = (half % 2) * HALF_SAMPLES
             result = out_pool.tile([P, C_OUT], F32, tag="result")
             nc.scalar.activation(out=result[:], in_=summed[half][:], func=RELU)
             nc.scalar.dma_start(
-                out=out[i, j, first : first + HALF_SAMPLES].rearrange("n y x c -> (n y x) c"), in_=result[:]
+                out=out[node_row, node_col, first : first + HALF_SAMPLES].rearrange("n y x o -> (n y x) o"),
+                in_=result[:],
             )
 
         for half in range(LOADS_AHEAD):
             load(half)
         for step in range(HALVES + 2):
-            if step >= 2:
-                half = step - 2
-                quantise_h(half, 1)
-                if half % 2 == 0:
-                    spread_bias(half // 2)
-                second_conv(half)
-                add_bias(half)
-                relu_and_store(half)
-            if step < HALVES:
+            preparing = step < HALVES
+            convolving = 1 <= step <= HALVES
+            finishing = step >= 2
+            if finishing:
+                quantise_h(step - 2, 1)
+            if preparing:
+                regroup_w(step, 1)
                 transpose_x(step)
-                for quarter in range(4):
-                    regroup_w(step, quarter)
-                for p in range(2):
-                    quantise_x(step, p)
-                for quarter in range(4):
-                    quantise_w(step, quarter)
+            if finishing:
+                if step % 2 == 0:
+                    spread_bias((step - 2) // 2)
+                second_conv(step - 2)
+            if preparing:
+                regroup_w(step, 0)
+                regroup_w(step, 2)
+                quantise_w(step, 0)
+                quantise_x(step, 0)
+                quantise_w(step, 2)
+                quantise_x(step, 1)
+                quantise_w(step, 1)
+            if finishing:
+                add_bias(step - 2)
+            if convolving:
+                for chunk in range(GROUP):
+                    first_conv(step - 1, chunk)
+            if finishing:
+                relu_and_store(step - 2)
+            if preparing:
+                regroup_w(step, 3)
                 if step + LOADS_AHEAD < HALVES:
                     load(step + LOADS_AHEAD)
-            if 1 <= step <= HALVES:
-                half = step - 1
-                for chunk in range(CHUNKS):
-                    first_conv(half, chunk)
-                    if chunk == 3:
-                        quantise_h(half, 0)
+            if convolving:
+                quantise_h(step - 1, 0)
+            if preparing:
+                quantise_w(step, 3)
+            if convolving:
+                for chunk in range(GROUP, CHUNKS):
+                    first_conv(step - 1, chunk)

from contextlib import ExitStack

import concourse.mybir as mybir
from concourse.masks import make_identity

BF16 = mybir.dt.bfloat16
F32 = mybir.dt.float32
U32 = mybir.dt.uint32
U8 = mybir.dt.uint8
FP8X4 = mybir.dt.float8_e4m3fn_x4
RELU = mybir.ActivationFunctionType.Relu
ADD = mybir.AluOpType.add

P = 128
PACK = 4
NODES = 4
HALVES = 2 * NODES
HALF_SAMPLES = 32
C_MID = 1024
C_OUT = 256
CHUNKS = C_MID // P
GROUP = 4
COLS = 512
RAW = 4096
QUARTERS = 4
QUARTER = 512
RUN = 4
LOADS_AHEAD = 3
SHARED_QUARTER = 1
SCALAR_GROUPS = 96

FLOPS = 2 * NODES * (1024 * 1024 * 1024 + 256 * 4096 * 256)


def tile_butterflylayer2d_pb_t_kernel(tc, x_leaf, f_first, b_first, f_second, b_second, out):
    nc = tc.nc
    with ExitStack() as ctx:
        consts = ctx.enter_context(tc.tile_pool(name="consts", bufs=1))
        raw_pool = ctx.enter_context(tc.tile_pool(name="raw", bufs=3 * LOADS_AHEAD))
        grouped_pool = ctx.enter_context(tc.tile_pool(name="grouped", bufs=QUARTERS))
        set_pool = ctx.enter_context(tc.tile_pool(name="sets", bufs=3))
        code_pool = ctx.enter_context(tc.tile_pool(name="codes", bufs=2))
        out_pool = ctx.enter_context(tc.tile_pool(name="outs", bufs=2))
        psum_x = ctx.enter_context(tc.psum_pool(name="psum_x", bufs=2))
        psum_h = ctx.enter_context(tc.psum_pool(name="psum_h", bufs=5))
        psum_out = ctx.enter_context(tc.psum_pool(name="psum_out", bufs=1))

        identity = consts.tile([P, P], F32)
        make_identity(nc, identity[:])

        bias_first = consts.tile([P, NODES * CHUNKS], BF16)
        with nc.allow_non_contiguous_dma(reason="a 8 KiB bias in runs of 4 values"):
            nc.scalar.dma_start(
                out=bias_first[:].rearrange("k (g lo) -> k g lo", lo=4),
                in_=b_first.rearrange("r s (hi k lo) -> k (r s hi) lo", hi=2, lo=4),
            )
        ones = consts.tile([P, P], BF16)
        nc.vector.memset(ones[:], 1.0)
        bias_row = consts.tile([P, NODES * C_OUT], BF16)
        nc.vector.memset(bias_row[:], 0.0)
        nc.scalar.dma_start(out=bias_row[0:1, :], in_=b_second.rearrange("(one r) s o -> one (r s o)", one=1))

        x_raw = {}
        w_raw = {}
        x_grouped = {}
        w_grouped = {}
        h_grouped = {}
        x_mx = {}
        w_mx = {}
        h_mx = {}
        bias_second = {}
        acc_out = {}
        summed = {}

        def load_weights(w_set, piece):
            node_row, node_col = divmod(w_set // 2, 2)
            rows = raw_pool.tile([P, RAW], BF16, tag="raw")
            if w_set % 2 == 0:
                nc.sync.dma_start(
                    out=rows[:].rearrange("k (q r) -> k q r", q=2),
                    in_=f_first[node_row, node_col, piece].rearrange("q (k e) m -> k q (e m)", e=2),
                )
            else:
                nc.sync.dma_start(
                    out=rows[:].rearrange("k (t r) -> k t r", t=PACK),
                    in_=f_second[node_row, node_col].rearrange(
                        "u v (hi k lo) o -> hi k (u v) (lo o)", hi=2, lo=4
                    )[piece],
                )
            w_raw[(w_set, piece)] = rows

        def load_x(half):
            node_row, node_col = divmod(half // 2, 2)
            first = (half % 2) * HALF_SAMPLES
            pixels = raw_pool.tile([P, RAW], BF16, tag="raw")
            nc.sync.dma_start(
                out=pixels[:],
                in_=x_leaf[node_row, node_col, first : first + HALF_SAMPLES].rearrange(
                    "n (Y p) X c -> (n Y) (p X c)", p=2
                ),
            )
            x_raw[half] = pixels

        def load(half):
            load_weights(half, 0)
            load_x(half)
            load_weights(half, 1)

        def transpose_x(half):
            words = x_raw[half][:].bitcast(F32)
            for p in range(2):
                grouped = grouped_pool.tile([P, PACK * COLS], BF16, tag="x_grouped", align_bytes=64)
                x_grouped[(half, p)] = grouped
                for x in range(2):
                    bank = psum_x.tile([P, 4, P], F32, tag="x_bank")
                    for a in range(4):
                        pixel = 8 * p + 4 * x + a
                        nc.tensor.transpose(bank[:, a, :], words[:, pixel * P : (pixel + 1) * P], identity[:])
                    nc.scalar.copy(
                        out=grouped[:]
                        .bitcast(F32)
                        .rearrange("k (ny x u a) -> k x ny u a", x=2, u=2, a=4)[:, x],
                        in_=bank[:].rearrange("k a (ny u) -> k ny u a", u=2),
                    )

        def quantise_x(half, p):
            if p == 0:
                codes = code_pool.tile([P, 2 * COLS], U32, tag="x_codes", align_bytes=64)
                scales = code_pool.tile([P, 2 * COLS], U8, tag="x_scales", align_bytes=64)
                x_mx[half] = (codes, scales)
            codes, scales = x_mx[half]
            cols = slice(p * COLS, (p + 1) * COLS)
            nc.vector.quantize_mx(
                out=codes[:, cols].bitcast(FP8X4), scales=scales[:, cols], in_=x_grouped[(half, p)][:]
            )

        def regroup_w(w_set, quarter):
            grouped = grouped_pool.tile([P, PACK * QUARTER], BF16, tag="w_grouped", align_bytes=64)
            w_grouped[quarter] = grouped
            rows = w_raw[(w_set, quarter // 2)][:].rearrange("k (t h g i) -> k h g t i", t=PACK, h=2, i=RUN)
            if w_set % 2 == 0:
                columns = grouped[:].rearrange("k (i g t) -> k g t i", i=RUN, t=PACK)
            else:
                columns = grouped[:].rearrange("k (g i t) -> k g t i", i=RUN, t=PACK)
            source = rows[:, quarter % 2]
            if quarter == SHARED_QUARTER:
                nc.scalar.copy(out=columns[:, :SCALAR_GROUPS], in_=source[:, :SCALAR_GROUPS])
                nc.vector.tensor_copy(out=columns[:, SCALAR_GROUPS:], in_=source[:, SCALAR_GROUPS:])
            else:
                nc.vector.tensor_copy(out=columns, in_=source)

        def quantise_w(w_set, quarter):
            if quarter == 0:
                codes = set_pool.tile([P, QUARTERS * QUARTER], U32, tag="w_codes", align_bytes=64)
                scales = set_pool.tile([P, QUARTERS * QUARTER], U8, tag="w_scales", align_bytes=64)
                w_mx[w_set] = (codes, scales)
            codes, scales = w_mx[w_set]
            cols = slice(quarter * QUARTER, (quarter + 1) * QUARTER)
            nc.vector.quantize_mx(
                out=codes[:, cols].bitcast(FP8X4), scales=scales[:, cols], in_=w_grouped[quarter][:]
            )

        def first_conv(half, chunk):
            node = half // 2
            w_codes, w_scales = w_mx[2 * node]
            x_codes, x_scales = x_mx[half]
            acc = psum_h.tile([P, COLS], F32, tag="acc_h")
            for p in range(2):
                w_cols = slice(p * C_MID + chunk * P, p * C_MID + (chunk + 1) * P)
                x_cols = slice(p * COLS, (p + 1) * COLS)
                nc.tensor.matmul_mx(
                    out=acc[:],
                    lhsT=w_codes[:, w_cols].bitcast(FP8X4),
                    lhsT_scale=w_scales[:, w_cols],
                    rhs=x_codes[:, x_cols].bitcast(FP8X4),
                    rhs_scale=x_scales[:, x_cols],
                    start=(p == 0),
                    stop=(p == 1),
                )
            if chunk % GROUP == 0:
                h_grouped[(half, chunk // GROUP)] = grouped_pool.tile(
                    [P, GROUP, COLS], BF16, tag="h_grouped", name="h_grouped", align_bytes=64
                )
            nc.scalar.activation(
                out=h_grouped[(half, chunk // GROUP)][:, chunk % GROUP, :],
                in_=acc[:],
                func=RELU,
                bias=bias_first[:, node * CHUNKS + chunk : node * CHUNKS + chunk + 1],
                scale=1.0,
            )

        def quantise_h(half, group):
            if group == 0:
                codes = code_pool.tile([P, CHUNKS * P], U32, tag="h_codes", align_bytes=64)
                scales = code_pool.tile([P, CHUNKS * P], U8, tag="h_scales", align_bytes=64)
                h_mx[half] = (codes, scales)
            codes, scales = h_mx[half]
            cols = slice(group * GROUP * P, (group + 1) * GROUP * P)
            nc.vector.quantize_mx(
                out=codes[:, cols].bitcast(FP8X4),
                scales=scales[:, cols],
                in_=h_grouped[(half, group)][:].rearrange("k chunk col -> k (chunk col)"),
            )

        def spread_bias(node):
            spread = psum_h.tile([P, COLS], F32, tag="acc_h")
            nc.tensor.matmul(
                out=spread[:, :C_OUT],
                lhsT=ones[:],
                rhs=bias_row[:, node * C_OUT : (node + 1) * C_OUT],
                start=True,
                stop=True,
            )
            bias_second[node] = out_pool.tile([P, C_OUT], F32, tag="bias_second", name="bias_second")
            nc.scalar.copy(out=bias_second[node][:], in_=spread[:, :C_OUT])

        def second_conv(half):
            h_codes, h_scales = h_mx[half]
            w_codes, w_scales = w_mx[2 * (half // 2) + 1]
            acc = psum_out.tile([P, C_OUT], F32, tag="acc_out")
            acc_out[half] = acc
            for chunk in range(CHUNKS):
                h_cols = slice(chunk * P, (chunk + 1) * P)
                w_cols = slice(chunk * C_OUT, (chunk + 1) * C_OUT)
                nc.tensor.matmul_mx(
                    out=acc[:],
                    lhsT=h_codes[:, h_cols].bitcast(FP8X4),
                    lhsT_scale=h_scales[:, h_cols],
                    rhs=w_codes[:, w_cols].bitcast(FP8X4),
                    rhs_scale=w_scales[:, w_cols],
                    start=(chunk == 0),
                    stop=(chunk == CHUNKS - 1),
                )

        def add_bias(half):
            node = half // 2
            summed[half] = out_pool.tile([P, C_OUT], F32, tag="summed", name="summed")
            nc.vector.tensor_tensor(
                out=summed[half][:],
                in0=acc_out[half][:],
                in1=bias_second[node][:],
                op=ADD,
            )

        def relu_and_store(half):
            node_row, node_col = divmod(half // 2, 2)
            first = (half % 2) * HALF_SAMPLES
            result = out_pool.tile([P, C_OUT], F32, tag="result")
            nc.scalar.activation(out=result[:], in_=summed[half][:], func=RELU)
            nc.scalar.dma_start(
                out=out[node_row, node_col, first : first + HALF_SAMPLES].rearrange("n y x o -> (n y x) o"),
                in_=result[:],
            )

        for half in range(LOADS_AHEAD):
            load(half)
        for step in range(HALVES + 2):
            preparing = step < HALVES
            convolving = 1 <= step <= HALVES
            finishing = step >= 2
            if finishing:
                quantise_h(step - 2, 1)
            if preparing:
                regroup_w(step, 1)
                transpose_x(step)
            if finishing:
                if step % 2 == 0:
                    spread_bias((step - 2) // 2)
                second_conv(step - 2)
            if preparing:
                regroup_w(step, 0)
                regroup_w(step, 2)
                quantise_w(step, 0)
                quantise_x(step, 0)
                quantise_w(step, 2)
                quantise_x(step, 1)
                quantise_w(step, 1)
            if finishing:
                add_bias(step - 2)
            if convolving:
                for chunk in range(GROUP):
                    first_conv(step - 1, chunk)
            if finishing:
                relu_and_store(step - 2)
            if preparing:
                regroup_w(step, 3)
                if step + LOADS_AHEAD < HALVES:
                    load(step + LOADS_AHEAD)
            if convolving:
                quantise_h(step - 1, 0)
            if preparing:
                quantise_w(step, 3)
            if convolving:
                for chunk in range(GROUP, CHUNKS):
                    first_conv(step - 1, chunk)
